import numpy as np
import ml_dtypes


def mxq(x, axis, fmt="e4m3"):
    dtype, down = {"e4m3": (ml_dtypes.float8_e4m3fn, 7), "e5m2": (ml_dtypes.float8_e5m2, 14)}[fmt]
    v = np.moveaxis(np.asarray(x, np.float32).astype(ml_dtypes.bfloat16).astype(np.float64), axis, -1)
    blocks = v.reshape(v.shape[:-1] + (-1, 32))
    amax = np.abs(blocks).max(-1, keepdims=True)
    byte = np.maximum(np.where(amax > 0, np.frexp(amax)[1] - 1 + 127, 0) - down, 1)
    scale = np.exp2(byte - 127.0)
    codes = (blocks / scale).astype(np.float32).astype(dtype).astype(np.float64)
    return np.moveaxis((codes * scale).reshape(v.shape), -1, axis)


WIDE = False


def mx_kscale(k):
    if not WIDE:
        return np.ones(k)
    levels = np.array([10, -10, 5, -5, 0])
    a = np.random.permutation(np.resize(levels, k // 512 * 4)).reshape(k // 512, 4)
    idx = np.arange(k)
    return np.exp2(a[idx // 512, idx % 128 // 32])


BF16 = ml_dtypes.bfloat16


def bf(x):
    return np.asarray(x, np.float32).astype(BF16)


def f64(x):
    return np.asarray(x).astype(np.float64)


M, K, N = 8192, 512, 512


def setup_inputs():
    s = mx_kscale(K)
    return {"A": bf(np.random.standard_normal((M, K)) * s),
            "B": bf(np.random.standard_normal((K, N)) * 2.0 / np.sqrt(K) / s[:, None])}


def reference(A, B):
    C = mxq(np.tril(f64(A)), 1, "e4m3") @ mxq(np.tril(f64(B)), 0, "e4m3")
    return np.tril(C)

@@ -1,0 +1,185 @@
+from contextlib import ExitStack
+
+import concourse.mybir as mybir
+from concourse.masks import make_identity
+
+M, K, N = 8192, 512, 512
+FLOPS = 2 * M * K * N
+
+BF16 = mybir.dt.bfloat16
+F32 = mybir.dt.float32
+U32 = mybir.dt.uint32
+U8 = mybir.dt.uint8
+FP8X4 = mybir.dt.float8_e4m3fn_x4
+MULT = mybir.AluOpType.mult
+IS_GE = mybir.AluOpType.is_ge
+
+P = 128
+GROUP = 4
+UNIT = 8
+CHUNKS = ((512, 4), (1024, 8), (0, 4), (2048, 16), (4096, 32))
+PINNED = True
+VECTOR_EVERY = 8
+
+
+def tile_modelnew_t_kernel(tc, A, B, out):
+    nc = tc.nc
+    with ExitStack() as ctx:
+        if PINNED:
+            ctx.enter_context(tc.manual_schedule())
+        const = ctx.enter_context(tc.tile_pool(name="const", bufs=1))
+        a_pool = ctx.enter_context(tc.tile_pool(name="a", bufs=1))
+        o_pool = ctx.enter_context(tc.tile_pool(name="o", bufs=6))
+        work = ctx.enter_context(tc.tile_pool(name="work", bufs=3))
+        xt_pool = ctx.enter_context(tc.psum_pool(name="xt", bufs=4))
+        acc_pool = ctx.enter_context(tc.psum_pool(name="acc", bufs=4))
+
+        a_tiles = []
+        b_raw = const.tile([P, 4, N], BF16)
+        for ci, (row0, tiles) in enumerate(CHUNKS):
+            a_sb = a_pool.tile([P, tiles * K], BF16, name="a%d" % ci)
+            nc.sync.dma_start(
+                out=a_sb[:],
+                in_=A[row0 : row0 + P * tiles, :].rearrange("(p t) k -> p (t k)", t=tiles),
+            )
+            a_tiles.append(a_sb)
+            if ci == 0:
+                nc.sync.dma_start(
+                    out=b_raw[:].rearrange("p (u e) c -> p u (e c)", u=2),
+                    in_=B.rearrange("(u q e) c -> q u (e c)", u=2, e=2),
+                )
+
+        b_mask = const.tile([P, N * 4], F32)
+        nc.vector.memset(b_mask[:], 1.0)
+        a_mask = const.tile([P, 4 * K], F32)
+        nc.vector.memset(a_mask[:], 1.0)
+        ident = const.tile([P, P], F32)
+        make_identity(nc, ident[:])
+        nc.gpsimd.affine_select(
+            out=b_mask[:], in_=b_mask[:], pattern=[[-1, N], [256, 2], [1, 2]],
+            compare_op=IS_GE, fill=0.0, base=0, channel_multiplier=2,
+        )
+        nc.gpsimd.affine_select(
+            out=a_mask[:], in_=a_mask[:], pattern=[[1, 4], [-1, K]],
+            compare_op=IS_GE, fill=0.0, base=0, channel_multiplier=4,
+        )
+
+        b_grp = const.tile([P, N * 4], BF16, align_bytes=64)
+        b_codes = const.tile([P, N], U32, align_bytes=64)
+        b_scl = const.tile([P, N], U8, align_bytes=64)
+
+        def prepare_b():
+            nc.vector.tensor_tensor(
+                out=b_grp[:].rearrange("p (c t) -> p c t", t=4),
+                in0=b_raw[:].rearrange("p t c -> p c t"),
+                in1=b_mask[:].rearrange("p (c t) -> p c t", t=4),
+                op=MULT,
+            )
+            nc.vector.quantize_mx(out=b_codes[:].bitcast(FP8X4), scales=b_scl[:], in_=b_grp[:])
+
+        groups = []
+        for ci, (row0, tiles) in enumerate(CHUNKS):
+            for t0 in range(0, tiles, GROUP):
+                groups.append((ci, t0))
+        n_groups = len(groups)
+        masked_group = [g for g in range(n_groups) if CHUNKS[groups[g][0]][0] == 0][0]
+        a_masked = const.tile([P, 4 * K], BF16)
+
+        state = {}
+        counter = [0]
+
+        def mask_a():
+            ci = groups[masked_group][0]
+            nc.vector.tensor_tensor(out=a_masked[:], in0=a_tiles[ci][:], in1=a_mask[:], op=MULT)
+
+        def transposes(g):
+            ci, t0 = groups[g]
+            src = a_masked if g == masked_group else a_tiles[ci]
+            words = src[:].bitcast(F32)
+            banks = []
+            for b in range(GROUP // 2):
+                xt = xt_pool.tile([P, 2, 2, P], F32, name="xt")
+                for r in range(2):
+                    for u in range(2):
+                        col = (t0 + 2 * b + r) * (K // 2) + u * P
+                        nc.tensor.transpose(xt[:, r, u, :], words[:, col : col + P], ident[:])
+                banks.append(xt)
+            state[("xt", g)] = banks
+
+        def regroup(g):
+            grp = work.tile([P, GROUP * P * 4], BF16, name="grp", align_bytes=64)
+            view = grp[:].bitcast(F32).rearrange("p (r m u) -> p r m u", r=GROUP, u=2)
+            for b, xt in enumerate(state[("xt", g)]):
+                nc.vector.tensor_copy(
+                    out=view[:, 2 * b : 2 * b + 2, :, :],
+                    in_=xt[:].rearrange("p r u m -> p r m u"),
+                )
+            state[("grp", g)] = grp
+
+        def quantise(g):
+            grp = state[("grp", g)]
+            codes = work.tile([P, GROUP * P], U32, name="codes", align_bytes=64)
+            scl = work.tile([P, GROUP * P], U8, name="scl", align_bytes=64)
+            nc.vector.quantize_mx(out=codes[:].bitcast(FP8X4), scales=scl[:], in_=grp[:])
+            state[("q", g)] = (codes, scl)
+
+        def multiply(g):
+            codes, scl = state[("q", g)]
+            accs = []
+            for r in range(GROUP):
+                acc = acc_pool.tile([P, N], F32, name="acc")
+                nc.tensor.matmul_mx(
+                    out=acc[:],
+                    lhsT=codes[:, r * P : (r + 1) * P].bitcast(FP8X4),
+                    lhsT_scale=scl[:, r * P : (r + 1) * P],
+                    rhs=b_codes[:].bitcast(FP8X4),
+                    rhs_scale=b_scl[:],
+                    start=True,
+                    stop=True,
+                )
+                accs.append(acc)
+            state[("acc", g)] = accs
+
+        def drain(g):
+            ci, t0 = groups[g]
+            row0, tiles = CHUNKS[ci]
+            unit = min(UNIT, tiles)
+            if t0 % unit == 0:
+                state["o"] = o_pool.tile([P, unit, N], F32, name="o_sb", tag="o")
+            o_sb = state["o"]
+            for r, acc in enumerate(state[("acc", g)]):
+                dst = o_sb[:, (t0 + r) % unit, :]
+                if g == masked_group:
+                    nc.vector.tensor_tensor(
+                        out=dst, in0=acc[:], in1=a_mask[:, (t0 + r) * K : (t0 + r + 1) * K], op=MULT
+                    )
+                else:
+                    counter[0] += 1
+                    if counter[0] % VECTOR_EVERY == 0:
+                        nc.vector.tensor_copy(out=dst, in_=acc[:])
+                    else:
+                        nc.scalar.copy(out=dst, in_=acc[:])
+            if (t0 + GROUP) % unit == 0:
+                first = t0 + GROUP - unit
+                nc.sync.dma_start(
+                    out=out[row0 : row0 + P * tiles, :].rearrange("(p t) n -> p t n", t=tiles)[
+                        :, first : first + unit, :
+                    ],
+                    in_=o_sb[:],
+                )
+
+        for s in range(n_groups + 2):
+            if s < n_groups:
+                transposes(s)
+            if s == 0:
+                prepare_b()
+            if 1 <= s <= n_groups:
+                quantise(s - 1)
+            if s >= 2:
+                multiply(s - 2)
+            if s < n_groups:
+                regroup(s)
+            if s + 2 == masked_group:
+                mask_a()
+            if s >= 2:
+                drain(s - 2)

@@ -12,14 +12,15 @@ U32 = mybir.dt.uint32
 U8 = mybir.dt.uint8
 FP8X4 = mybir.dt.float8_e4m3fn_x4
 MULT = mybir.AluOpType.mult
-IS_GE = mybir.AluOpType.is_ge
+IS_LE = mybir.AluOpType.is_le
 
 P = 128
 GROUP = 4
 UNIT = 8
-CHUNKS = ((512, 4), (1024, 8), (0, 4), (2048, 16), (4096, 32))
+CHUNKS = ((512, 4), (1024, 8), (2048, 16), (4096, 32), (0, 4))
 PINNED = True
-VECTOR_EVERY = 8
+VECTOR_EVERY = 16
+MASK_SLOT = 10
 
 
 def tile_modelnew_t_kernel(tc, A, B, out):
@@ -36,6 +37,7 @@ def tile_modelnew_t_kernel(tc, A, B, out):
 
         a_tiles = []
         b_raw = const.tile([P, 4, N], BF16)
+        half = N // 2
         for ci, (row0, tiles) in enumerate(CHUNKS):
             a_sb = a_pool.tile([P, tiles * K], BF16, name="a%d" % ci)
             nc.sync.dma_start(
@@ -45,23 +47,26 @@ def tile_modelnew_t_kernel(tc, A, B, out):
             a_tiles.append(a_sb)
             if ci == 0:
                 nc.sync.dma_start(
-                    out=b_raw[:].rearrange("p (u e) c -> p u (e c)", u=2),
-                    in_=B.rearrange("(u q e) c -> q u (e c)", u=2, e=2),
+                    out=b_raw[:, 0:2, 0:half],
+                    in_=B[0:half, 0:half].rearrange("(q e) c -> q e c", e=2),
+                )
+                nc.sync.dma_start(
+                    out=b_raw[:, 2:4, :],
+                    in_=B[half:K, :].rearrange("(q e) c -> q e c", e=2),
                 )
 
-        b_mask = const.tile([P, N * 4], F32)
-        nc.vector.memset(b_mask[:], 1.0)
-        a_mask = const.tile([P, 4 * K], F32)
-        nc.vector.memset(a_mask[:], 1.0)
+        nc.vector.memset(b_raw[:, 0:2, half:N], 0.0)
         ident = const.tile([P, P], F32)
         make_identity(nc, ident[:])
-        nc.gpsimd.affine_select(
-            out=b_mask[:], in_=b_mask[:], pattern=[[-1, N], [256, 2], [1, 2]],
-            compare_op=IS_GE, fill=0.0, base=0, channel_multiplier=2,
+        b_diff = const.tile([P, 2, half], F32)
+        nc.gpsimd.iota(
+            b_diff[:], pattern=[[-1, 2], [1, half]], base=0, channel_multiplier=-2,
+            allow_small_or_imprecise_dtypes=True,
         )
-        nc.gpsimd.affine_select(
-            out=a_mask[:], in_=a_mask[:], pattern=[[1, 4], [-1, K]],
-            compare_op=IS_GE, fill=0.0, base=0, channel_multiplier=4,
+        a_diff = const.tile([P, K], F32)
+        nc.gpsimd.iota(
+            a_diff[:], pattern=[[1, K]], base=0, channel_multiplier=-4,
+            allow_small_or_imprecise_dtypes=True,
         )
 
         b_grp = const.tile([P, N * 4], BF16, align_bytes=64)
@@ -69,11 +74,14 @@ def tile_modelnew_t_kernel(tc, A, B, out):
         b_scl = const.tile([P, N], U8, align_bytes=64)
 
         def prepare_b():
-            nc.vector.tensor_tensor(
+            for u in range(2):
+                corner = b_raw[:, 2 * u : 2 * u + 2, u * half : (u + 1) * half]
+                nc.vector.scalar_tensor_tensor(
+                    out=corner, in0=b_diff[:], scalar=0.0, in1=corner, op0=IS_LE, op1=MULT
+                )
+            nc.vector.tensor_copy(
                 out=b_grp[:].rearrange("p (c t) -> p c t", t=4),
-                in0=b_raw[:].rearrange("p t c -> p c t"),
-                in1=b_mask[:].rearrange("p (c t) -> p c t", t=4),
-                op=MULT,
+                in_=b_raw[:].rearrange("p t c -> p c t"),
             )
             nc.vector.quantize_mx(out=b_codes[:].bitcast(FP8X4), scales=b_scl[:], in_=b_grp[:])
 
@@ -88,9 +96,12 @@ def tile_modelnew_t_kernel(tc, A, B, out):
         state = {}
         counter = [0]
 
-        def mask_a():
+        def mask_a(t):
             ci = groups[masked_group][0]
-            nc.vector.tensor_tensor(out=a_masked[:], in0=a_tiles[ci][:], in1=a_mask[:], op=MULT)
+            nc.vector.scalar_tensor_tensor(
+                out=a_masked[:, t * K : (t + 1) * K], in0=a_diff[:], scalar=float(t),
+                in1=a_tiles[ci][:, t * K : (t + 1) * K], op0=IS_LE, op1=MULT,
+            )
 
         def transposes(g):
             ci, t0 = groups[g]
@@ -149,16 +160,11 @@ def tile_modelnew_t_kernel(tc, A, B, out):
             o_sb = state["o"]
             for r, acc in enumerate(state[("acc", g)]):
                 dst = o_sb[:, (t0 + r) % unit, :]
-                if g == masked_group:
-                    nc.vector.tensor_tensor(
-                        out=dst, in0=acc[:], in1=a_mask[:, (t0 + r) * K : (t0 + r + 1) * K], op=MULT
-                    )
+                counter[0] += 1
+                if counter[0] % VECTOR_EVERY == 0:
+                    nc.vector.tensor_copy(out=dst, in_=acc[:])
                 else:
-                    counter[0] += 1
-                    if counter[0] % VECTOR_EVERY == 0:
-                        nc.vector.tensor_copy(out=dst, in_=acc[:])
-                    else:
-                        nc.scalar.copy(out=dst, in_=acc[:])
+                    nc.scalar.copy(out=dst, in_=acc[:])
             if (t0 + GROUP) % unit == 0:
                 first = t0 + GROUP - unit
                 nc.sync.dma_start(
@@ -171,15 +177,15 @@ def tile_modelnew_t_kernel(tc, A, B, out):
         for s in range(n_groups + 2):
             if s < n_groups:
                 transposes(s)
-            if s == 0:
-                prepare_b()
             if 1 <= s <= n_groups:
                 quantise(s - 1)
             if s >= 2:
                 multiply(s - 2)
             if s < n_groups:
                 regroup(s)
-            if s + 2 == masked_group:
-                mask_a()
+            if s == 0:
+                prepare_b()
+            if MASK_SLOT <= s < MASK_SLOT + 4:
+                mask_a(s - MASK_SLOT)
             if s >= 2:
                 drain(s - 2)

@@ -18,7 +18,7 @@ P = 128
 GROUP = 4
 UNIT = 8
 CHUNKS = ((512, 4), (1024, 8), (2048, 16), (4096, 32), (0, 4))
-PINNED = True
+PINNED = False
 VECTOR_EVERY = 16
 MASK_SLOT = 10
 

@@ -16,10 +16,11 @@ IS_LE = mybir.AluOpType.is_le
 
 P = 128
 GROUP = 4
-UNIT = 8
+STORES = ((4,), (8,), (8, 8), (8, 8, 8, 8), (4,))
 CHUNKS = ((512, 4), (1024, 8), (2048, 16), (4096, 32), (0, 4))
-PINNED = False
-VECTOR_EVERY = 16
+PINNED = True
+VECTOR_EVERY = 8
+HEAD_ON_SCALAR = 2
 MASK_SLOT = 10
 
 
@@ -30,7 +31,7 @@ def tile_modelnew_t_kernel(tc, A, B, out):
             ctx.enter_context(tc.manual_schedule())
         const = ctx.enter_context(tc.tile_pool(name="const", bufs=1))
         a_pool = ctx.enter_context(tc.tile_pool(name="a", bufs=1))
-        o_pool = ctx.enter_context(tc.tile_pool(name="o", bufs=6))
+        o_pool = ctx.enter_context(tc.tile_pool(name="o", bufs=1))
         work = ctx.enter_context(tc.tile_pool(name="work", bufs=3))
         xt_pool = ctx.enter_context(tc.psum_pool(name="xt", bufs=4))
         acc_pool = ctx.enter_context(tc.psum_pool(name="acc", bufs=4))
@@ -38,6 +39,14 @@ def tile_modelnew_t_kernel(tc, A, B, out):
         a_tiles = []
         b_raw = const.tile([P, 4, N], BF16)
         half = N // 2
+        nc.sync.dma_start(
+            out=b_raw[:, 0:2, 0:half],
+            in_=B[0:half, 0:half].rearrange("(q e) c -> q e c", e=2),
+        )
+        nc.sync.dma_start(
+            out=b_raw[:, 2:4, :],
+            in_=B[half:K, :].rearrange("(q e) c -> q e c", e=2),
+        )
         for ci, (row0, tiles) in enumerate(CHUNKS):
             a_sb = a_pool.tile([P, tiles * K], BF16, name="a%d" % ci)
             nc.sync.dma_start(
@@ -45,24 +54,15 @@ def tile_modelnew_t_kernel(tc, A, B, out):
                 in_=A[row0 : row0 + P * tiles, :].rearrange("(p t) k -> p (t k)", t=tiles),
             )
             a_tiles.append(a_sb)
-            if ci == 0:
-                nc.sync.dma_start(
-                    out=b_raw[:, 0:2, 0:half],
-                    in_=B[0:half, 0:half].rearrange("(q e) c -> q e c", e=2),
-                )
-                nc.sync.dma_start(
-                    out=b_raw[:, 2:4, :],
-                    in_=B[half:K, :].rearrange("(q e) c -> q e c", e=2),
-                )
 
         nc.vector.memset(b_raw[:, 0:2, half:N], 0.0)
-        ident = const.tile([P, P], F32)
-        make_identity(nc, ident[:])
         b_diff = const.tile([P, 2, half], F32)
         nc.gpsimd.iota(
             b_diff[:], pattern=[[-1, 2], [1, half]], base=0, channel_multiplier=-2,
             allow_small_or_imprecise_dtypes=True,
         )
+        ident = const.tile([P, P], F32)
+        make_identity(nc, ident[:])
         a_diff = const.tile([P, K], F32)
         nc.gpsimd.iota(
             a_diff[:], pattern=[[1, K]], base=0, channel_multiplier=-4,
@@ -121,10 +121,11 @@ def tile_modelnew_t_kernel(tc, A, B, out):
             grp = work.tile([P, GROUP * P * 4], BF16, name="grp", align_bytes=64)
             view = grp[:].bitcast(F32).rearrange("p (r m u) -> p r m u", r=GROUP, u=2)
             for b, xt in enumerate(state[("xt", g)]):
-                nc.vector.tensor_copy(
-                    out=view[:, 2 * b : 2 * b + 2, :, :],
-                    in_=xt[:].rearrange("p r u m -> p r m u"),
-                )
+                dst = view[:, 2 * b : 2 * b + 2, :, :]
+                if g < HEAD_ON_SCALAR:
+                    nc.scalar.copy(out=dst, in_=xt[:].rearrange("p r u m -> p r m u"))
+                else:
+                    nc.vector.tensor_copy(out=dst, in_=xt[:].rearrange("p r u m -> p r m u"))
             state[("grp", g)] = grp
 
         def quantise(g):
@@ -154,19 +155,25 @@ def tile_modelnew_t_kernel(tc, A, B, out):
         def drain(g):
             ci, t0 = groups[g]
             row0, tiles = CHUNKS[ci]
-            unit = min(UNIT, tiles)
-            if t0 % unit == 0:
-                state["o"] = o_pool.tile([P, unit, N], F32, name="o_sb", tag="o")
+            first = 0
+            unit = STORES[ci][0]
+            for width in STORES[ci]:
+                if first + width <= t0:
+                    first += width
+                else:
+                    unit = width
+                    break
+            if t0 == first:
+                state["o"] = o_pool.tile([P, unit, N], F32, name="o%d_%d" % (ci, first))
             o_sb = state["o"]
             for r, acc in enumerate(state[("acc", g)]):
-                dst = o_sb[:, (t0 + r) % unit, :]
+                dst = o_sb[:, t0 + r - first, :]
                 counter[0] += 1
                 if counter[0] % VECTOR_EVERY == 0:
                     nc.vector.tensor_copy(out=dst, in_=acc[:])
                 else:
                     nc.scalar.copy(out=dst, in_=acc[:])
-            if (t0 + GROUP) % unit == 0:
-                first = t0 + GROUP - unit
+            if t0 + GROUP == first + unit:
                 nc.sync.dma_start(
                     out=out[row0 : row0 + P * tiles, :].rearrange("(p t) n -> p t n", t=tiles)[
                         :, first : first + unit, :
@@ -174,6 +181,7 @@ def tile_modelnew_t_kernel(tc, A, B, out):
                     in_=o_sb[:],
                 )
 
+        prepare_b()
         for s in range(n_groups + 2):
             if s < n_groups:
                 transposes(s)
@@ -183,8 +191,6 @@ def tile_modelnew_t_kernel(tc, A, B, out):
                 multiply(s - 2)
             if s < n_groups:
                 regroup(s)
-            if s == 0:
-                prepare_b()
             if MASK_SLOT <= s < MASK_SLOT + 4:
                 mask_a(s - MASK_SLOT)
             if s >= 2:

@@ -16,7 +16,7 @@ IS_LE = mybir.AluOpType.is_le
 
 P = 128
 GROUP = 4
-STORES = ((4,), (8,), (8, 8), (8, 8, 8, 8), (4,))
+STORES = ((4,), (8,), (16,), (16, 16), (4,))
 CHUNKS = ((512, 4), (1024, 8), (2048, 16), (4096, 32), (0, 4))
 PINNED = True
 VECTOR_EVERY = 8

from contextlib import ExitStack

import concourse.mybir as mybir
from concourse.masks import make_identity

M, K, N = 8192, 512, 512
FLOPS = 2 * M * K * N

BF16 = mybir.dt.bfloat16
F32 = mybir.dt.float32
U32 = mybir.dt.uint32
U8 = mybir.dt.uint8
FP8X4 = mybir.dt.float8_e4m3fn_x4
MULT = mybir.AluOpType.mult
IS_LE = mybir.AluOpType.is_le

P = 128
GROUP = 4
STORES = ((4,), (8,), (16,), (16, 16), (4,))
CHUNKS = ((512, 4), (1024, 8), (2048, 16), (4096, 32), (0, 4))
PINNED = True
VECTOR_EVERY = 8
HEAD_ON_SCALAR = 2
MASK_SLOT = 10


def tile_modelnew_t_kernel(tc, A, B, out):
    nc = tc.nc
    with ExitStack() as ctx:
        if PINNED:
            ctx.enter_context(tc.manual_schedule())
        const = ctx.enter_context(tc.tile_pool(name="const", bufs=1))
        a_pool = ctx.enter_context(tc.tile_pool(name="a", bufs=1))
        o_pool = ctx.enter_context(tc.tile_pool(name="o", bufs=1))
        work = ctx.enter_context(tc.tile_pool(name="work", bufs=3))
        xt_pool = ctx.enter_context(tc.psum_pool(name="xt", bufs=4))
        acc_pool = ctx.enter_context(tc.psum_pool(name="acc", bufs=4))

        a_tiles = []
        b_raw = const.tile([P, 4, N], BF16)
        half = N // 2
        nc.sync.dma_start(
            out=b_raw[:, 0:2, 0:half],
            in_=B[0:half, 0:half].rearrange("(q e) c -> q e c", e=2),
        )
        nc.sync.dma_start(
            out=b_raw[:, 2:4, :],
            in_=B[half:K, :].rearrange("(q e) c -> q e c", e=2),
        )
        for ci, (row0, tiles) in enumerate(CHUNKS):
            a_sb = a_pool.tile([P, tiles * K], BF16, name="a%d" % ci)
            nc.sync.dma_start(
                out=a_sb[:],
                in_=A[row0 : row0 + P * tiles, :].rearrange("(p t) k -> p (t k)", t=tiles),
            )
            a_tiles.append(a_sb)

        nc.vector.memset(b_raw[:, 0:2, half:N], 0.0)
        b_diff = const.tile([P, 2, half], F32)
        nc.gpsimd.iota(
            b_diff[:], pattern=[[-1, 2], [1, half]], base=0, channel_multiplier=-2,
            allow_small_or_imprecise_dtypes=True,
        )
        ident = const.tile([P, P], F32)
        make_identity(nc, ident[:])
        a_diff = const.tile([P, K], F32)
        nc.gpsimd.iota(
            a_diff[:], pattern=[[1, K]], base=0, channel_multiplier=-4,
            allow_small_or_imprecise_dtypes=True,
        )

        b_grp = const.tile([P, N * 4], BF16, align_bytes=64)
        b_codes = const.tile([P, N], U32, align_bytes=64)
        b_scl = const.tile([P, N], U8, align_bytes=64)

        def prepare_b():
            for u in range(2):
                corner = b_raw[:, 2 * u : 2 * u + 2, u * half : (u + 1) * half]
                nc.vector.scalar_tensor_tensor(
                    out=corner, in0=b_diff[:], scalar=0.0, in1=corner, op0=IS_LE, op1=MULT
                )
            nc.vector.tensor_copy(
                out=b_grp[:].rearrange("p (c t) -> p c t", t=4),
                in_=b_raw[:].rearrange("p t c -> p c t"),
            )
            nc.vector.quantize_mx(out=b_codes[:].bitcast(FP8X4), scales=b_scl[:], in_=b_grp[:])

        groups = []
        for ci, (row0, tiles) in enumerate(CHUNKS):
            for t0 in range(0, tiles, GROUP):
                groups.append((ci, t0))
        n_groups = len(groups)
        masked_group = [g for g in range(n_groups) if CHUNKS[groups[g][0]][0] == 0][0]
        a_masked = const.tile([P, 4 * K], BF16)

        state = {}
        counter = [0]

        def mask_a(t):
            ci = groups[masked_group][0]
            nc.vector.scalar_tensor_tensor(
                out=a_masked[:, t * K : (t + 1) * K], in0=a_diff[:], scalar=float(t),
                in1=a_tiles[ci][:, t * K : (t + 1) * K], op0=IS_LE, op1=MULT,
            )

        def transposes(g):
            ci, t0 = groups[g]
            src = a_masked if g == masked_group else a_tiles[ci]
            words = src[:].bitcast(F32)
            banks = []
            for b in range(GROUP // 2):
                xt = xt_pool.tile([P, 2, 2, P], F32, name="xt")
                for r in range(2):
                    for u in range(2):
                        col = (t0 + 2 * b + r) * (K // 2) + u * P
                        nc.tensor.transpose(xt[:, r, u, :], words[:, col : col + P], ident[:])
                banks.append(xt)
            state[("xt", g)] = banks

        def regroup(g):
            grp = work.tile([P, GROUP * P * 4], BF16, name="grp", align_bytes=64)
            view = grp[:].bitcast(F32).rearrange("p (r m u) -> p r m u", r=GROUP, u=2)
            for b, xt in enumerate(state[("xt", g)]):
                dst = view[:, 2 * b : 2 * b + 2, :, :]
                if g < HEAD_ON_SCALAR:
                    nc.scalar.copy(out=dst, in_=xt[:].rearrange("p r u m -> p r m u"))
                else:
                    nc.vector.tensor_copy(out=dst, in_=xt[:].rearrange("p r u m -> p r m u"))
            state[("grp", g)] = grp

        def quantise(g):
            grp = state[("grp", g)]
            codes = work.tile([P, GROUP * P], U32, name="codes", align_bytes=64)
            scl = work.tile([P, GROUP * P], U8, name="scl", align_bytes=64)
            nc.vector.quantize_mx(out=codes[:].bitcast(FP8X4), scales=scl[:], in_=grp[:])
            state[("q", g)] = (codes, scl)

        def multiply(g):
            codes, scl = state[("q", g)]
            accs = []
            for r in range(GROUP):
                acc = acc_pool.tile([P, N], F32, name="acc")
                nc.tensor.matmul_mx(
                    out=acc[:],
                    lhsT=codes[:, r * P : (r + 1) * P].bitcast(FP8X4),
                    lhsT_scale=scl[:, r * P : (r + 1) * P],
                    rhs=b_codes[:].bitcast(FP8X4),
                    rhs_scale=b_scl[:],
                    start=True,
                    stop=True,
                )
                accs.append(acc)
            state[("acc", g)] = accs

        def drain(g):
            ci, t0 = groups[g]
            row0, tiles = CHUNKS[ci]
            first = 0
            unit = STORES[ci][0]
            for width in STORES[ci]:
                if first + width <= t0:
                    first += width
                else:
                    unit = width
                    break
            if t0 == first:
                state["o"] = o_pool.tile([P, unit, N], F32, name="o%d_%d" % (ci, first))
            o_sb = state["o"]
            for r, acc in enumerate(state[("acc", g)]):
                dst = o_sb[:, t0 + r - first, :]
                counter[0] += 1
                if counter[0] % VECTOR_EVERY == 0:
                    nc.vector.tensor_copy(out=dst, in_=acc[:])
                else:
                    nc.scalar.copy(out=dst, in_=acc[:])
            if t0 + GROUP == first + unit:
                nc.sync.dma_start(
                    out=out[row0 : row0 + P * tiles, :].rearrange("(p t) n -> p t n", t=tiles)[
                        :, first : first + unit, :
                    ],
                    in_=o_sb[:],
                )

        prepare_b()
        for s in range(n_groups + 2):
            if s < n_groups:
                transposes(s)
            if 1 <= s <= n_groups:
                quantise(s - 1)
            if s >= 2:
                multiply(s - 2)
            if s < n_groups:
                regroup(s)
            if MASK_SLOT <= s < MASK_SLOT + 4:
                mask_a(s - MASK_SLOT)
            if s >= 2:
                drain(s - 2)
